import numpy as np
import ml_dtypes


def mxq(x, axis, fmt="e4m3"):
    dtype, down = {"e4m3": (ml_dtypes.float8_e4m3fn, 7), "e5m2": (ml_dtypes.float8_e5m2, 14)}[fmt]
    v = np.moveaxis(np.asarray(x, np.float32).astype(ml_dtypes.bfloat16).astype(np.float64), axis, -1)
    blocks = v.reshape(v.shape[:-1] + (-1, 32))
    amax = np.abs(blocks).max(-1, keepdims=True)
    byte = np.maximum(np.where(amax > 0, np.frexp(amax)[1] - 1 + 127, 0) - down, 1)
    scale = np.exp2(byte - 127.0)
    codes = (blocks / scale).astype(np.float32).astype(dtype).astype(np.float64)
    return np.moveaxis((codes * scale).reshape(v.shape), -1, axis)


WIDE = False


def mx_kscale(k):
    if not WIDE:
        return np.ones(k)
    levels = np.array([10, -10, 5, -5, 0])
    a = np.random.permutation(np.resize(levels, k // 512 * 4)).reshape(k // 512, 4)
    idx = np.arange(k)
    return np.exp2(a[idx // 512, idx % 128 // 32])


BF16 = ml_dtypes.bfloat16


def bf(x):
    return np.asarray(x, np.float32).astype(BF16)


def f64(x):
    return np.asarray(x).astype(np.float64)


E2M1 = np.array([0.0, 0.5, 1.0, 1.5, 2.0, 3.0, 4.0, 6.0, -0.0, -0.5, -1.0, -1.5, -2.0, -3.0, -4.0, -6.0])


def pack_weight(w, fmt):
    k, n = w.shape
    w = f64(bf(w)).reshape(k // 32, 32, n)
    amax = np.abs(w).max(1)
    if fmt == "e4m3":
        byte = np.frexp(amax)[1] - 1 + 127 - 7
    else:
        mant, ex = np.frexp(amax / 6.0)
        byte = np.where(mant > 0.5, ex, ex - 1) + 127
    byte = np.clip(np.where(amax > 0, byte, 1), 1, 254)
    scaled = (w * np.exp2(127.0 - byte)[:, None, :]).reshape(k, n).astype(np.float32)
    by_word = np.ascontiguousarray(scaled.reshape(k // 512, 128, 4, n).transpose(0, 1, 3, 2))
    if fmt == "e4m3":
        words = by_word.astype(ml_dtypes.float8_e4m3fn).view(np.uint8)
    else:
        c = by_word.astype(ml_dtypes.float4_e2m1fn).view(np.uint8) & 0xF
        words = c[..., 0::2] | (c[..., 1::2] << 4)
    return np.ascontiguousarray(words), np.ascontiguousarray(byte.astype(np.uint8).reshape(k // 512, 16, n))


def unpack_weight(words, scales, fmt):
    g, p, n, _ = words.shape
    if fmt == "e4m3":
        vals = np.ascontiguousarray(words).view(ml_dtypes.float8_e4m3fn).astype(np.float64)
    else:
        nib = np.empty((g, p, n, 4), np.uint8)
        nib[..., 0::2] = words & 0xF
        nib[..., 1::2] = words >> 4
        vals = E2M1[nib]
    vals = vals * np.repeat(np.exp2(scales.astype(np.float64) - 127.0), 8, axis=1)[..., None]
    return vals.transpose(0, 1, 3, 2).reshape(g * 512, n)

def pack4(w):
    words, scales = pack_weight(w, "e2m1")
    return words.reshape(words.shape[0], 128, -1), scales


def unpack4(words, scales):
    return unpack_weight(words.reshape(words.shape[0], 128, -1, 2), scales, "e2m1")


N, C, H = 128, 1024, 16
D = C // H
SIN_TIME = 10000.0


def create_sinusoidal_positions(n_pos, dim, time):
    denom = np.power(time, 2 * (np.arange(dim) // 2) / dim)
    position_enc = np.arange(n_pos)[:, None] / denom[None, :]
    return np.concatenate([np.sin(position_enc[:, 0::2]), np.cos(position_enc[:, 1::2])], axis=-1)


def apply_rope(x, time):
    pos = create_sinusoidal_positions(x.shape[-2], x.shape[-1], time)
    sin, cos = np.split(pos, 2, axis=-1)
    sin_pos = np.stack([sin, sin], axis=-1).reshape(pos.shape)
    cos_pos = np.stack([cos, cos], axis=-1).reshape(pos.shape)
    rotated = np.stack([-x[..., 1::2], x[..., ::2]], axis=-1).reshape(x.shape)
    return x * cos_pos + rotated * sin_pos


def setup_inputs():
    s = mx_kscale(C)
    x = bf(np.random.standard_normal((N, C)) * s)
    w = np.random.standard_normal((2 * C, C)) / np.sqrt(C) / s[None, :]
    words, scales = pack4(np.ascontiguousarray(w.T))
    return {"x": x, "W_qk_words": words, "W_qk_scales": scales}


def reference(x, W_qk_words, W_qk_scales):
    qk = mxq(f64(x), 1, "e4m3") @ unpack4(W_qk_words, W_qk_scales)
    qk = qk.reshape(N, 2, H, D).transpose(1, 2, 0, 3)
    q, k = qk[0], qk[1]
    return apply_rope(q, SIN_TIME), apply_rope(k, SIN_TIME)

@@ -1,0 +1,182 @@
+import math
+
+import concourse.mybir as mybir
+from concourse.masks import make_identity
+
+F32 = mybir.dt.float32
+BF16 = mybir.dt.bfloat16
+I32 = mybir.dt.int32
+U32 = mybir.dt.uint32
+U8 = mybir.dt.uint8
+FP8X4 = mybir.dt.float8_e4m3fn_x4
+FP4X4 = mybir.dt.float4_e2m1fn_x4
+ALU = mybir.AluOpType
+ACT = mybir.ActivationFunctionType
+
+P = 128
+K = 1024
+PACK = 4
+K_PASS = P * PACK
+PASSES = K // K_PASS
+COLS = 2048
+BANK = 512
+BANKS = COLS // BANK
+HEAD = 64
+PAIRS = HEAD // 2
+HEADS_IN_BANK = BANK // HEAD
+BANKS_PER_OUTPUT = BANKS // 2
+HALF = BANK // 2
+
+ROPE_BASE = 10000.0
+ROUND_MAGIC = 12582912.0
+
+FLOPS = 2 * P * K * COLS
+
+
+def build_rotation_table(nc, pool):
+    position = pool.tile([P, 1], F32)
+    nc.gpsimd.iota(
+        position[:],
+        pattern=[[0, 1]],
+        base=0,
+        channel_multiplier=1,
+        allow_small_or_imprecise_dtypes=True,
+    )
+    turns = pool.tile([P, 3, PAIRS], F32)
+    ratio = ROPE_BASE ** (-1.0 / PAIRS)
+    nc.vector.tensor_scalar_mul(
+        out=turns[:, 2, 0:1], in0=position[:], scalar1=1.0 / (2.0 * math.pi)
+    )
+    width = 1
+    while width < PAIRS:
+        nc.vector.tensor_scalar_mul(
+            out=turns[:, 2, width : 2 * width],
+            in0=turns[:, 2, 0:width],
+            scalar1=ratio**width,
+        )
+        width *= 2
+    nc.vector.tensor_scalar_add(out=turns[:, 1, :], in0=turns[:, 2, :], scalar1=0.25)
+    nc.vector.tensor_scalar_add(out=turns[:, 0, :], in0=turns[:, 2, :], scalar1=0.5)
+    whole = pool.tile([P, 3, PAIRS], F32)
+    nc.vector.tensor_scalar(
+        out=whole[:],
+        in0=turns[:],
+        scalar1=ROUND_MAGIC,
+        scalar2=ROUND_MAGIC,
+        op0=ALU.add,
+        op1=ALU.subtract,
+    )
+    part = pool.tile([P, 3, PAIRS], F32)
+    nc.vector.tensor_tensor(out=part[:], in0=turns[:], in1=whole[:], op=ALU.subtract)
+    trig = pool.tile([P, 3, PAIRS], F32)
+    nc.scalar.activation(out=trig[:], in_=part[:], func=ACT.Sin, scale=2.0 * math.pi)
+    return trig
+
+
+def tile_attentionblock_pa_s_kernel(tc, x, W_qk_words, W_qk_scales, out_0, out_1):
+    nc = tc.nc
+    with (
+        tc.tile_pool(name="keep", bufs=1) as keep,
+        tc.tile_pool(name="work", bufs=BANKS) as work,
+        tc.psum_pool(name="psum", bufs=1) as psum,
+    ):
+        x_sb = keep.tile([P, PASSES, K_PASS], BF16)
+        for g in range(PASSES):
+            nc.sync.dma_start(out=x_sb[:, g, :], in_=x[:, K_PASS * g : K_PASS * (g + 1)])
+
+        w_words = keep.tile([P, BANKS, PASSES, 2 * BANK], U8, align_bytes=64)
+
+        def load_words(b):
+            nc.sync.dma_start(
+                out=w_words[:, b, :, :].bitcast(I32),
+                in_=W_qk_words[:, :, 2 * BANK * b : 2 * BANK * (b + 1)]
+                .bitcast(I32)
+                .rearrange("g p c -> p g c"),
+            )
+
+        load_words(0)
+
+        w_scales = keep.tile([P, PASSES, COLS], U8, align_bytes=64)
+        nc.vector.memset(w_scales[:].bitcast(I32), 0)
+        scale_rows = W_qk_scales.bitcast(I32)
+        for r in range(4):
+            nc.sync.dma_start(
+                out=w_scales[r:P:32].bitcast(I32),
+                in_=scale_rows[:, r:16:4, :].rearrange("g q n -> q g n"),
+            )
+
+        for b in range(1, BANKS):
+            load_words(b)
+
+        trig = build_rotation_table(nc, keep)
+        identity = keep.tile([P, P], F32)
+        make_identity(nc, identity[:])
+
+        x_pairs = x_sb[:].bitcast(F32)
+        grouped = keep.tile([P, PASSES, P * PACK], BF16, align_bytes=64)
+        x_codes = keep.tile([P, PASSES, P], U32, align_bytes=64)
+        x_scales = keep.tile([P, PASSES, P], U8, align_bytes=64)
+        for g in range(PASSES):
+            flipped = psum.tile([P, 2, P], F32, name="flipped%d" % g)
+            for u in range(2):
+                nc.tensor.transpose(
+                    flipped[:, u, :],
+                    x_pairs[:, g, u : K_PASS // 2 : 2],
+                    identity[:],
+                )
+            side_by_side = grouped[:, g, :].bitcast(F32).rearrange("p (n u) -> p n u", u=2)
+            alternately = flipped[:].rearrange("p u n -> p n u")
+            if g == 0:
+                nc.vector.tensor_copy(out=side_by_side, in_=alternately)
+            else:
+                nc.scalar.copy(out=side_by_side, in_=alternately)
+        for g in range(PASSES):
+            nc.vector.quantize_mx(
+                out=x_codes[:, g, :].bitcast(FP8X4),
+                scales=x_scales[:, g, :],
+                in_=grouped[:, g, :],
+            )
+
+        for b in range(BANKS):
+            y = psum.tile([P, BANK], F32, name="y%d" % b)
+            for g in range(PASSES):
+                nc.tensor.matmul_mx(
+                    out=y[:],
+                    lhsT=x_codes[:, g, :].bitcast(FP8X4),
+                    lhsT_scale=x_scales[:, g, :],
+                    rhs=w_words[:, b, g, :].bitcast(FP4X4),
+                    rhs_scale=w_scales[:, g, BANK * b : BANK * (b + 1)],
+                    start=(g == 0),
+                    stop=(g == PASSES - 1),
+                )
+
+            shape = [P, 2, HEADS_IN_BANK, PAIRS]
+            halves = y[:].rearrange("p (h i e) -> p e h i", i=PAIRS, e=2)
+            products = work.tile([P, 4, HALF], F32)
+            planes = products[:].rearrange("p t (h i) -> p t h i", i=PAIRS)
+            nc.vector.tensor_tensor(
+                out=planes[:, 1:3],
+                in0=halves[:, 0:1].to_broadcast(shape),
+                in1=trig[:, 1:3, :].unsqueeze(2).to_broadcast(shape),
+                op=ALU.mult,
+            )
+            nc.vector.tensor_tensor(
+                out=planes[:, 0:4:3],
+                in0=halves[:, 1:2].to_broadcast(shape),
+                in1=trig[:, 0:2, :].unsqueeze(2).to_broadcast(shape),
+                op=ALU.mult,
+            )
+            rotated = work.tile([P, BANK], F32)
+            adder = nc.gpsimd if b < BANKS_PER_OUTPUT else nc.vector
+            adder.tensor_tensor(
+                out=rotated[:].rearrange("p (m e) -> p m e", e=2),
+                in0=products[:, 0:4:2, :].rearrange("p e m -> p m e"),
+                in1=products[:, 1:4:2, :].rearrange("p e m -> p m e"),
+                op=ALU.add,
+            )
+            out = out_0 if b < BANKS_PER_OUTPUT else out_1
+            first_head = HEADS_IN_BANK * (b % BANKS_PER_OUTPUT)
+            nc.sync.dma_start(
+                out=out[first_head : first_head + HEADS_IN_BANK].rearrange("h n d -> n h d"),
+                in_=rotated[:].rearrange("n (h d) -> n h d", d=HEAD),
+            )

@@ -79,7 +79,11 @@ def tile_attentionblock_pa_s_kernel(tc, x, W_qk_words, W_qk_scales, out_0, out_1
         tc.tile_pool(name="keep", bufs=1) as keep,
         tc.tile_pool(name="work", bufs=BANKS) as work,
         tc.psum_pool(name="psum", bufs=1) as psum,
+        tc.manual_schedule(),
     ):
+        w_scales = keep.tile([P, PASSES, COLS], U8, align_bytes=64)
+        nc.vector.memset(w_scales[:].bitcast(I32), 0)
+
         x_sb = keep.tile([P, PASSES, K_PASS], BF16)
         for g in range(PASSES):
             nc.sync.dma_start(out=x_sb[:, g, :], in_=x[:, K_PASS * g : K_PASS * (g + 1)])
@@ -96,8 +100,6 @@ def tile_attentionblock_pa_s_kernel(tc, x, W_qk_words, W_qk_scales, out_0, out_1
 
         load_words(0)
 
-        w_scales = keep.tile([P, PASSES, COLS], U8, align_bytes=64)
-        nc.vector.memset(w_scales[:].bitcast(I32), 0)
         scale_rows = W_qk_scales.bitcast(I32)
         for r in range(4):
             nc.sync.dma_start(
@@ -108,9 +110,9 @@ def tile_attentionblock_pa_s_kernel(tc, x, W_qk_words, W_qk_scales, out_0, out_1
         for b in range(1, BANKS):
             load_words(b)
 
-        trig = build_rotation_table(nc, keep)
         identity = keep.tile([P, P], F32)
         make_identity(nc, identity[:])
+        trig = build_rotation_table(nc, keep)
 
         x_pairs = x_sb[:].bitcast(F32)
         grouped = keep.tile([P, PASSES, P * PACK], BF16, align_bytes=64)
@@ -137,6 +139,7 @@ def tile_attentionblock_pa_s_kernel(tc, x, W_qk_words, W_qk_scales, out_0, out_1
                 in_=grouped[:, g, :],
             )
 
+        y_banks = []
         for b in range(BANKS):
             y = psum.tile([P, BANK], F32, name="y%d" % b)
             for g in range(PASSES):
@@ -149,10 +152,12 @@ def tile_attentionblock_pa_s_kernel(tc, x, W_qk_words, W_qk_scales, out_0, out_1
                     start=(g == 0),
                     stop=(g == PASSES - 1),
                 )
+            y_banks.append(y)
 
+        def multiply(b):
             shape = [P, 2, HEADS_IN_BANK, PAIRS]
-            halves = y[:].rearrange("p (h i e) -> p e h i", i=PAIRS, e=2)
-            products = work.tile([P, 4, HALF], F32)
+            halves = y_banks[b][:].rearrange("p (h i e) -> p e h i", i=PAIRS, e=2)
+            products = work.tile([P, 4, HALF], F32, name="products")
             planes = products[:].rearrange("p t (h i) -> p t h i", i=PAIRS)
             nc.vector.tensor_tensor(
                 out=planes[:, 1:3],
@@ -166,8 +171,10 @@ def tile_attentionblock_pa_s_kernel(tc, x, W_qk_words, W_qk_scales, out_0, out_1
                 in1=trig[:, 0:2, :].unsqueeze(2).to_broadcast(shape),
                 op=ALU.mult,
             )
-            rotated = work.tile([P, BANK], F32)
-            adder = nc.gpsimd if b < BANKS_PER_OUTPUT else nc.vector
+            return products
+
+        def add_and_store(adder, b, products):
+            rotated = work.tile([P, BANK], F32, name="rotated")
             adder.tensor_tensor(
                 out=rotated[:].rearrange("p (m e) -> p m e", e=2),
                 in0=products[:, 0:4:2, :].rearrange("p e m -> p m e"),
@@ -180,3 +187,11 @@ def tile_attentionblock_pa_s_kernel(tc, x, W_qk_words, W_qk_scales, out_0, out_1
                 out=out[first_head : first_head + HEADS_IN_BANK].rearrange("h n d -> n h d"),
                 in_=rotated[:].rearrange("n (h d) -> n h d", d=HEAD),
             )
+
+        all_products = []
+        for b in range(BANKS):
+            all_products.append(multiply(b))
+            if b < BANKS_PER_OUTPUT:
+                add_and_store(nc.gpsimd, b, all_products[b])
+        for b in range(BANKS_PER_OUTPUT, BANKS):
+            add_and_store(nc.vector, b, all_products[b])

@@ -30,34 +30,25 @@ HALF = BANK // 2
 ROPE_BASE = 10000.0
 ROUND_MAGIC = 12582912.0
 
+FIRST = 8
+IDLE_MATMULS = 3
+
 FLOPS = 2 * P * K * COLS
 
 
-def build_rotation_table(nc, pool):
-    position = pool.tile([P, 1], F32)
-    nc.gpsimd.iota(
-        position[:],
-        pattern=[[0, 1]],
-        base=0,
-        channel_multiplier=1,
-        allow_small_or_imprecise_dtypes=True,
-    )
-    turns = pool.tile([P, 3, PAIRS], F32)
+def build_rotation_table(nc, pool, position):
+    turns = pool.tile([P, 2, PAIRS], F32)
     ratio = ROPE_BASE ** (-1.0 / PAIRS)
-    nc.vector.tensor_scalar_mul(
-        out=turns[:, 2, 0:1], in0=position[:], scalar1=1.0 / (2.0 * math.pi)
-    )
-    width = 1
-    while width < PAIRS:
+    for i in range(FIRST):
         nc.vector.tensor_scalar_mul(
-            out=turns[:, 2, width : 2 * width],
-            in0=turns[:, 2, 0:width],
-            scalar1=ratio**width,
+            out=turns[:, 1, i : i + 1], in0=position[:], scalar1=ratio**i / (2.0 * math.pi)
         )
-        width *= 2
-    nc.vector.tensor_scalar_add(out=turns[:, 1, :], in0=turns[:, 2, :], scalar1=0.25)
-    nc.vector.tensor_scalar_add(out=turns[:, 0, :], in0=turns[:, 2, :], scalar1=0.5)
-    whole = pool.tile([P, 3, PAIRS], F32)
+    for i in range(FIRST, PAIRS, FIRST):
+        nc.vector.tensor_scalar_mul(
+            out=turns[:, 1, i : i + FIRST], in0=turns[:, 1, 0:FIRST], scalar1=ratio**i
+        )
+    nc.vector.tensor_scalar_add(out=turns[:, 0, :], in0=turns[:, 1, :], scalar1=0.25)
+    whole = pool.tile([P, 2, PAIRS], F32)
     nc.vector.tensor_scalar(
         out=whole[:],
         in0=turns[:],
@@ -66,10 +57,11 @@ def build_rotation_table(nc, pool):
         op0=ALU.add,
         op1=ALU.subtract,
     )
-    part = pool.tile([P, 3, PAIRS], F32)
+    part = pool.tile([P, 2, PAIRS], F32)
     nc.vector.tensor_tensor(out=part[:], in0=turns[:], in1=whole[:], op=ALU.subtract)
     trig = pool.tile([P, 3, PAIRS], F32)
-    nc.scalar.activation(out=trig[:], in_=part[:], func=ACT.Sin, scale=2.0 * math.pi)
+    nc.scalar.activation(out=trig[:, 1:3, :], in_=part[:], func=ACT.Sin, scale=2.0 * math.pi)
+    nc.scalar.activation(out=trig[:, 0, :], in_=part[:, 1, :], func=ACT.Sin, scale=-2.0 * math.pi)
     return trig
 
 
@@ -81,6 +73,15 @@ def tile_attentionblock_pa_s_kernel(tc, x, W_qk_words, W_qk_scales, out_0, out_1
         tc.psum_pool(name="psum", bufs=1) as psum,
         tc.manual_schedule(),
     ):
+        position = keep.tile([P, 1], F32)
+        nc.gpsimd.iota(
+            position[:],
+            pattern=[[0, 1]],
+            base=0,
+            channel_multiplier=1,
+            allow_small_or_imprecise_dtypes=True,
+        )
+
         w_scales = keep.tile([P, PASSES, COLS], U8, align_bytes=64)
         nc.vector.memset(w_scales[:].bitcast(I32), 0)
 
@@ -110,9 +111,15 @@ def tile_attentionblock_pa_s_kernel(tc, x, W_qk_words, W_qk_scales, out_0, out_1
         for b in range(1, BANKS):
             load_words(b)
 
+        zeros = keep.tile([P, P], F32)
+        nc.gpsimd.memset(zeros[:], 0.0)
+        unread = psum.tile([P, P], F32)
+        for idle in range(IDLE_MATMULS):
+            nc.tensor.matmul(out=unread[:], lhsT=zeros[:], rhs=zeros[:], start=True, stop=True)
+
         identity = keep.tile([P, P], F32)
         make_identity(nc, identity[:])
-        trig = build_rotation_table(nc, keep)
+        trig = build_rotation_table(nc, keep, position)
 
         x_pairs = x_sb[:].bitcast(F32)
         grouped = keep.tile([P, PASSES, P * PACK], BF16, align_bytes=64)

@@ -25,11 +25,15 @@ HEAD = 64
 PAIRS = HEAD // 2
 HEADS_IN_BANK = BANK // HEAD
 BANKS_PER_OUTPUT = BANKS // 2
-HALF = BANK // 2
 
 ROPE_BASE = 10000.0
 ROUND_MAGIC = 12582912.0
 
+HEADS = COLS // 2 // HEAD
+PIECE_HEADS = 4
+PIECE = PIECE_HEADS * HEAD
+PIECES = COLS // PIECE
+ROUNDS = ((2, 2), (1, 2), (0, 1))
 FIRST = 8
 IDLE_MATMULS = 3
 
@@ -59,17 +63,27 @@ def build_rotation_table(nc, pool, position):
     )
     part = pool.tile([P, 2, PAIRS], F32)
     nc.vector.tensor_tensor(out=part[:], in0=turns[:], in1=whole[:], op=ALU.subtract)
-    trig = pool.tile([P, 3, PAIRS], F32)
-    nc.scalar.activation(out=trig[:, 1:3, :], in_=part[:], func=ACT.Sin, scale=2.0 * math.pi)
-    nc.scalar.activation(out=trig[:, 0, :], in_=part[:, 1, :], func=ACT.Sin, scale=-2.0 * math.pi)
-    return trig
+    table = pool.tile([P, 2, PAIRS, 2], F32)
+    nc.scalar.activation(
+        out=table[:, 0, :, :],
+        in_=part[:, 0, :].unsqueeze(2).to_broadcast([P, PAIRS, 2]),
+        func=ACT.Sin,
+        scale=2.0 * math.pi,
+    )
+    nc.scalar.activation(
+        out=table[:, 1, :, 0], in_=part[:, 1, :], func=ACT.Sin, scale=2.0 * math.pi
+    )
+    nc.scalar.activation(
+        out=table[:, 1, :, 1], in_=part[:, 1, :], func=ACT.Sin, scale=-2.0 * math.pi
+    )
+    return table
 
 
 def tile_attentionblock_pa_s_kernel(tc, x, W_qk_words, W_qk_scales, out_0, out_1):
     nc = tc.nc
     with (
         tc.tile_pool(name="keep", bufs=1) as keep,
-        tc.tile_pool(name="work", bufs=BANKS) as work,
+        tc.tile_pool(name="work", bufs=PIECES) as work,
         tc.psum_pool(name="psum", bufs=1) as psum,
         tc.manual_schedule(),
     ):
@@ -119,7 +133,7 @@ def tile_attentionblock_pa_s_kernel(tc, x, W_qk_words, W_qk_scales, out_0, out_1
 
         identity = keep.tile([P, P], F32)
         make_identity(nc, identity[:])
-        trig = build_rotation_table(nc, keep, position)
+        table = build_rotation_table(nc, keep, position)
 
         x_pairs = x_sb[:].bitcast(F32)
         grouped = keep.tile([P, PASSES, P * PACK], BF16, align_bytes=64)
@@ -161,44 +175,45 @@ def tile_attentionblock_pa_s_kernel(tc, x, W_qk_words, W_qk_scales, out_0, out_1
                 )
             y_banks.append(y)
 
-        def multiply(b):
-            shape = [P, 2, HEADS_IN_BANK, PAIRS]
-            halves = y_banks[b][:].rearrange("p (h i e) -> p e h i", i=PAIRS, e=2)
-            products = work.tile([P, 4, HALF], F32, name="products")
-            planes = products[:].rearrange("p t (h i) -> p t h i", i=PAIRS)
+        def multiply(piece):
+            b, first = divmod(PIECE_HEADS * piece, HEADS_IN_BANK)
+            shape = [P, 2, PIECE_HEADS, HEAD]
+            products = work.tile([P, 2, PIECE], F32, name="products")
             nc.vector.tensor_tensor(
-                out=planes[:, 1:3],
-                in0=halves[:, 0:1].to_broadcast(shape),
-                in1=trig[:, 1:3, :].unsqueeze(2).to_broadcast(shape),
-                op=ALU.mult,
-            )
-            nc.vector.tensor_tensor(
-                out=planes[:, 0:4:3],
-                in0=halves[:, 1:2].to_broadcast(shape),
-                in1=trig[:, 0:2, :].unsqueeze(2).to_broadcast(shape),
+                out=products[:].rearrange("p t (h d) -> p t h d", d=HEAD),
+                in0=y_banks[b][:, HEAD * first : HEAD * first + PIECE]
+                .rearrange("p (h d) -> p h d", d=HEAD)
+                .unsqueeze(1)
+                .to_broadcast(shape),
+                in1=table[:].rearrange("p t i e -> p t (i e)").unsqueeze(2).to_broadcast(shape),
                 op=ALU.mult,
             )
             return products
 
-        def add_and_store(adder, b, products):
-            rotated = work.tile([P, BANK], F32, name="rotated")
+        def add_and_store(adder, piece, products):
+            rotated = work.tile([P, PIECE], F32, name="rotated")
             adder.tensor_tensor(
                 out=rotated[:].rearrange("p (m e) -> p m e", e=2),
-                in0=products[:, 0:4:2, :].rearrange("p e m -> p m e"),
-                in1=products[:, 1:4:2, :].rearrange("p e m -> p m e"),
+                in0=products[:, 0, :].rearrange("p (m e) -> p m e", e=2),
+                in1=products[:, 1, :].rearrange("p (m e) -> p m e", e=2)[:, :, ::-1],
                 op=ALU.add,
             )
-            out = out_0 if b < BANKS_PER_OUTPUT else out_1
-            first_head = HEADS_IN_BANK * (b % BANKS_PER_OUTPUT)
+            which, first_head = divmod(PIECE_HEADS * piece, HEADS)
+            out = (out_0, out_1)[which]
             nc.sync.dma_start(
-                out=out[first_head : first_head + HEADS_IN_BANK].rearrange("h n d -> n h d"),
+                out=out[first_head : first_head + PIECE_HEADS].rearrange("h n d -> n h d"),
                 in_=rotated[:].rearrange("n (h d) -> n h d", d=HEAD),
             )
 
-        all_products = []
-        for b in range(BANKS):
-            all_products.append(multiply(b))
-            if b < BANKS_PER_OUTPUT:
-                add_and_store(nc.gpsimd, b, all_products[b])
-        for b in range(BANKS_PER_OUTPUT, BANKS):
-            add_and_store(nc.vector, b, all_products[b])
+        piece = 0
+        for for_gpsimd, for_vector in ROUNDS:
+            waiting = []
+            for turn in range(for_gpsimd + for_vector):
+                products = multiply(piece)
+                if turn < for_gpsimd:
+                    add_and_store(nc.gpsimd, piece, products)
+                else:
+                    waiting.append((piece, products))
+                piece += 1
+            for late_piece, products in waiting:
+                add_and_store(nc.vector, late_piece, products)

@@ -30,10 +30,8 @@ ROPE_BASE = 10000.0
 ROUND_MAGIC = 12582912.0
 
 HEADS = COLS // 2 // HEAD
-PIECE_HEADS = 4
-PIECE = PIECE_HEADS * HEAD
-PIECES = COLS // PIECE
-ROUNDS = ((2, 2), (1, 2), (0, 1))
+ROUNDS = ((4, 2, 2), (4, 1, 2), (2, 0, 2))
+PIECES = 9
 FIRST = 8
 IDLE_MATMULS = 3
 
@@ -175,13 +173,13 @@ def tile_attentionblock_pa_s_kernel(tc, x, W_qk_words, W_qk_scales, out_0, out_1
                 )
             y_banks.append(y)
 
-        def multiply(piece):
-            b, first = divmod(PIECE_HEADS * piece, HEADS_IN_BANK)
-            shape = [P, 2, PIECE_HEADS, HEAD]
-            products = work.tile([P, 2, PIECE], F32, name="products")
+        def multiply(first_head, heads):
+            b, first = divmod(first_head, HEADS_IN_BANK)
+            shape = [P, 2, heads, HEAD]
+            products = work.tile([P, 2, heads * HEAD], F32, name="products")
             nc.vector.tensor_tensor(
                 out=products[:].rearrange("p t (h d) -> p t h d", d=HEAD),
-                in0=y_banks[b][:, HEAD * first : HEAD * first + PIECE]
+                in0=y_banks[b][:, HEAD * first : HEAD * (first + heads)]
                 .rearrange("p (h d) -> p h d", d=HEAD)
                 .unsqueeze(1)
                 .to_broadcast(shape),
@@ -190,30 +188,30 @@ def tile_attentionblock_pa_s_kernel(tc, x, W_qk_words, W_qk_scales, out_0, out_1
             )
             return products
 
-        def add_and_store(adder, piece, products):
-            rotated = work.tile([P, PIECE], F32, name="rotated")
+        def add_and_store(adder, first_head, heads, products):
+            rotated = work.tile([P, heads * HEAD], F32, name="rotated")
             adder.tensor_tensor(
                 out=rotated[:].rearrange("p (m e) -> p m e", e=2),
                 in0=products[:, 0, :].rearrange("p (m e) -> p m e", e=2),
                 in1=products[:, 1, :].rearrange("p (m e) -> p m e", e=2)[:, :, ::-1],
                 op=ALU.add,
             )
-            which, first_head = divmod(PIECE_HEADS * piece, HEADS)
+            which, head = divmod(first_head, HEADS)
             out = (out_0, out_1)[which]
             nc.sync.dma_start(
-                out=out[first_head : first_head + PIECE_HEADS].rearrange("h n d -> n h d"),
+                out=out[head : head + heads].rearrange("h n d -> n h d"),
                 in_=rotated[:].rearrange("n (h d) -> n h d", d=HEAD),
             )
 
-        piece = 0
-        for for_gpsimd, for_vector in ROUNDS:
+        first_head = 0
+        for heads, for_gpsimd, for_vector in ROUNDS:
             waiting = []
             for turn in range(for_gpsimd + for_vector):
-                products = multiply(piece)
+                products = multiply(first_head, heads)
                 if turn < for_gpsimd:
-                    add_and_store(nc.gpsimd, piece, products)
+                    add_and_store(nc.gpsimd, first_head, heads, products)
                 else:
-                    waiting.append((piece, products))
-                piece += 1
-            for late_piece, products in waiting:
-                add_and_store(nc.vector, late_piece, products)
+                    waiting.append((first_head, products))
+                first_head += heads
+            for late_head, products in waiting:
+                add_and_store(nc.vector, late_head, heads, products)

@@ -33,7 +33,8 @@ HEADS = COLS // 2 // HEAD
 ROUNDS = ((4, 2, 2), (4, 1, 2), (2, 0, 2))
 PIECES = 9
 FIRST = 8
-IDLE_MATMULS = 3
+IDLE_BEFORE_X = 4
+IDLE_BEFORE_CODES = 2
 
 FLOPS = 2 * P * K * COLS
 
@@ -94,6 +95,9 @@ def tile_attentionblock_pa_s_kernel(tc, x, W_qk_words, W_qk_scales, out_0, out_1
             allow_small_or_imprecise_dtypes=True,
         )
 
+        zeros = keep.tile([P, P], F32)
+        nc.vector.memset(zeros[:], 0.0)
+
         w_scales = keep.tile([P, PASSES, COLS], U8, align_bytes=64)
         nc.vector.memset(w_scales[:].bitcast(I32), 0)
 
@@ -123,11 +127,13 @@ def tile_attentionblock_pa_s_kernel(tc, x, W_qk_words, W_qk_scales, out_0, out_1
         for b in range(1, BANKS):
             load_words(b)
 
-        zeros = keep.tile([P, P], F32)
-        nc.gpsimd.memset(zeros[:], 0.0)
         unread = psum.tile([P, P], F32)
-        for idle in range(IDLE_MATMULS):
-            nc.tensor.matmul(out=unread[:], lhsT=zeros[:], rhs=zeros[:], start=True, stop=True)
+
+        def idle_matmuls(count):
+            for idle in range(count):
+                nc.tensor.matmul(out=unread[:], lhsT=zeros[:], rhs=zeros[:], start=True, stop=True)
+
+        idle_matmuls(IDLE_BEFORE_X)
 
         identity = keep.tile([P, P], F32)
         make_identity(nc, identity[:])
@@ -151,6 +157,7 @@ def tile_attentionblock_pa_s_kernel(tc, x, W_qk_words, W_qk_scales, out_0, out_1
                 nc.vector.tensor_copy(out=side_by_side, in_=alternately)
             else:
                 nc.scalar.copy(out=side_by_side, in_=alternately)
+        idle_matmuls(IDLE_BEFORE_CODES)
         for g in range(PASSES):
             nc.vector.quantize_mx(
                 out=x_codes[:, g, :].bitcast(FP8X4),

@@ -30,8 +30,9 @@ ROPE_BASE = 10000.0
 ROUND_MAGIC = 12582912.0
 
 HEADS = COLS // 2 // HEAD
-ROUNDS = ((4, 2, 2), (4, 1, 2), (2, 0, 2))
-PIECES = 9
+FIRST_GROUP = 2 * HEAD
+ROUNDS = ((2, 2, 0), (4, 1, 2), (4, 1, 2), (2, 0, 2))
+PIECES = 10
 FIRST = 8
 IDLE_BEFORE_X = 4
 IDLE_BEFORE_CODES = 2
@@ -107,15 +108,16 @@ def tile_attentionblock_pa_s_kernel(tc, x, W_qk_words, W_qk_scales, out_0, out_1
 
         w_words = keep.tile([P, BANKS, PASSES, 2 * BANK], U8, align_bytes=64)
 
-        def load_words(b):
+        def load_words(first, width):
+            b, in_bank = divmod(first, BANK)
             nc.sync.dma_start(
-                out=w_words[:, b, :, :].bitcast(I32),
-                in_=W_qk_words[:, :, 2 * BANK * b : 2 * BANK * (b + 1)]
+                out=w_words[:, b, :, 2 * in_bank : 2 * (in_bank + width)].bitcast(I32),
+                in_=W_qk_words[:, :, 2 * first : 2 * (first + width)]
                 .bitcast(I32)
                 .rearrange("g p c -> p g c"),
             )
 
-        load_words(0)
+        load_words(0, FIRST_GROUP)
 
         scale_rows = W_qk_scales.bitcast(I32)
         for r in range(4):
@@ -124,8 +126,9 @@ def tile_attentionblock_pa_s_kernel(tc, x, W_qk_words, W_qk_scales, out_0, out_1
                 in_=scale_rows[:, r:16:4, :].rearrange("g q n -> q g n"),
             )
 
+        load_words(FIRST_GROUP, BANK - FIRST_GROUP)
         for b in range(1, BANKS):
-            load_words(b)
+            load_words(BANK * b, BANK)
 
         unread = psum.tile([P, P], F32)
 
@@ -165,28 +168,48 @@ def tile_attentionblock_pa_s_kernel(tc, x, W_qk_words, W_qk_scales, out_0, out_1
                 in_=grouped[:, g, :],
             )
 
-        y_banks = []
-        for b in range(BANKS):
+        def project(y, first, width, g):
+            b, in_bank = divmod(first, BANK)
+            nc.tensor.matmul_mx(
+                out=y,
+                lhsT=x_codes[:, g, :].bitcast(FP8X4),
+                lhsT_scale=x_scales[:, g, :],
+                rhs=w_words[:, b, g, 2 * in_bank : 2 * (in_bank + width)].bitcast(FP4X4),
+                rhs_scale=w_scales[:, g, first : first + width],
+                start=(g == 0),
+                stop=(g == PASSES - 1),
+            )
+
+        y_first = psum.tile([P, FIRST_GROUP], F32)
+        y_rest = psum.tile([P, BANK - FIRST_GROUP], F32)
+        project(y_first[:], 0, FIRST_GROUP, 0)
+        project(y_rest[:, 0:FIRST_GROUP], FIRST_GROUP, FIRST_GROUP, 0)
+        project(y_first[:], 0, FIRST_GROUP, 1)
+        project(y_rest[:, 0:FIRST_GROUP], FIRST_GROUP, FIRST_GROUP, 1)
+        for first in range(2 * FIRST_GROUP, BANK, FIRST_GROUP):
+            for g in range(PASSES):
+                project(y_rest[:, first - FIRST_GROUP : first], first, FIRST_GROUP, g)
+        y_banks = [None]
+        for b in range(1, BANKS):
             y = psum.tile([P, BANK], F32, name="y%d" % b)
             for g in range(PASSES):
-                nc.tensor.matmul_mx(
-                    out=y[:],
-                    lhsT=x_codes[:, g, :].bitcast(FP8X4),
-                    lhsT_scale=x_scales[:, g, :],
-                    rhs=w_words[:, b, g, :].bitcast(FP4X4),
-                    rhs_scale=w_scales[:, g, BANK * b : BANK * (b + 1)],
-                    start=(g == 0),
-                    stop=(g == PASSES - 1),
-                )
+                project(y[:], BANK * b, BANK, g)
             y_banks.append(y)
 
+        def y_columns(first, width):
+            if first < FIRST_GROUP:
+                return y_first[:, first : first + width]
+            if first < BANK:
+                return y_rest[:, first - FIRST_GROUP : first - FIRST_GROUP + width]
+            b, in_bank = divmod(first, BANK)
+            return y_banks[b][:, in_bank : in_bank + width]
+
         def multiply(first_head, heads):
-            b, first = divmod(first_head, HEADS_IN_BANK)
             shape = [P, 2, heads, HEAD]
             products = work.tile([P, 2, heads * HEAD], F32, name="products")
             nc.vector.tensor_tensor(
                 out=products[:].rearrange("p t (h d) -> p t h d", d=HEAD),
-                in0=y_banks[b][:, HEAD * first : HEAD * (first + heads)]
+                in0=y_columns(HEAD * first_head, HEAD * heads)
                 .rearrange("p (h d) -> p h d", d=HEAD)
                 .unsqueeze(1)
                 .to_broadcast(shape),

@@ -40,7 +40,7 @@ IDLE_BEFORE_CODES = 2
 FLOPS = 2 * P * K * COLS
 
 
-def build_rotation_table(nc, pool, position):
+def build_angles(nc, pool, position):
     turns = pool.tile([P, 2, PAIRS], F32)
     ratio = ROPE_BASE ** (-1.0 / PAIRS)
     for i in range(FIRST):
@@ -63,6 +63,10 @@ def build_rotation_table(nc, pool, position):
     )
     part = pool.tile([P, 2, PAIRS], F32)
     nc.vector.tensor_tensor(out=part[:], in0=turns[:], in1=whole[:], op=ALU.subtract)
+    return part
+
+
+def build_rotation_table(nc, pool, part):
     table = pool.tile([P, 2, PAIRS, 2], F32)
     nc.scalar.activation(
         out=table[:, 0, :, :],
@@ -140,7 +144,9 @@ def tile_attentionblock_pa_s_kernel(tc, x, W_qk_words, W_qk_scales, out_0, out_1
 
         identity = keep.tile([P, P], F32)
         make_identity(nc, identity[:])
-        table = build_rotation_table(nc, keep, position)
+        part = build_angles(nc, keep, position)
+        unused = keep.tile([P, 1], F32)
+        nc.scalar.activation(out=unused[:], in_=position[:], func=ACT.Sin, scale=0.0)
 
         x_pairs = x_sb[:].bitcast(F32)
         grouped = keep.tile([P, PASSES, P * PACK], BF16, align_bytes=64)
@@ -161,6 +167,7 @@ def tile_attentionblock_pa_s_kernel(tc, x, W_qk_words, W_qk_scales, out_0, out_1
             else:
                 nc.scalar.copy(out=side_by_side, in_=alternately)
         idle_matmuls(IDLE_BEFORE_CODES)
+        table = build_rotation_table(nc, keep, part)
         for g in range(PASSES):
             nc.vector.quantize_mx(
                 out=x_codes[:, g, :].bitcast(FP8X4),

@@ -103,8 +103,10 @@ def tile_attentionblock_pa_s_kernel(tc, x, W_qk_words, W_qk_scales, out_0, out_1
         zeros = keep.tile([P, P], F32)
         nc.vector.memset(zeros[:], 0.0)
 
-        w_scales = keep.tile([P, PASSES, COLS], U8, align_bytes=64)
-        nc.vector.memset(w_scales[:].bitcast(I32), 0)
+        w_scales_first = keep.tile([P, PASSES, BANK], U8, align_bytes=64)
+        w_scales_rest = keep.tile([P, PASSES, COLS - BANK], U8, align_bytes=64)
+        nc.vector.memset(w_scales_first[:].bitcast(I32), 0)
+        nc.vector.memset(w_scales_rest[:].bitcast(I32), 0)
 
         x_sb = keep.tile([P, PASSES, K_PASS], BF16)
         for g in range(PASSES):
@@ -123,14 +125,18 @@ def tile_attentionblock_pa_s_kernel(tc, x, W_qk_words, W_qk_scales, out_0, out_1
 
         load_words(0, FIRST_GROUP)
 
-        scale_rows = W_qk_scales.bitcast(I32)
-        for r in range(4):
-            nc.sync.dma_start(
-                out=w_scales[r:P:32].bitcast(I32),
-                in_=scale_rows[:, r:16:4, :].rearrange("g q n -> q g n"),
-            )
+        def load_scales(planes, first, width):
+            for r in range(4):
+                nc.sync.dma_start(
+                    out=planes[r:P:32].bitcast(I32),
+                    in_=W_qk_scales[:, r:16:4, first : first + width]
+                    .bitcast(I32)
+                    .rearrange("g q n -> q g n"),
+                )
 
+        load_scales(w_scales_first, 0, BANK)
         load_words(FIRST_GROUP, BANK - FIRST_GROUP)
+        load_scales(w_scales_rest, BANK, COLS - BANK)
         for b in range(1, BANKS):
             load_words(BANK * b, BANK)
 
@@ -177,12 +183,13 @@ def tile_attentionblock_pa_s_kernel(tc, x, W_qk_words, W_qk_scales, out_0, out_1
 
         def project(y, first, width, g):
             b, in_bank = divmod(first, BANK)
+            planes, offset = (w_scales_first, 0) if b == 0 else (w_scales_rest, BANK)
             nc.tensor.matmul_mx(
                 out=y,
                 lhsT=x_codes[:, g, :].bitcast(FP8X4),
                 lhsT_scale=x_scales[:, g, :],
                 rhs=w_words[:, b, g, 2 * in_bank : 2 * (in_bank + width)].bitcast(FP4X4),
-                rhs_scale=w_scales[:, g, first : first + width],
+                rhs_scale=planes[:, g, first - offset : first - offset + width],
                 start=(g == 0),
                 stop=(g == PASSES - 1),
             )

@@ -103,10 +103,11 @@ def tile_attentionblock_pa_s_kernel(tc, x, W_qk_words, W_qk_scales, out_0, out_1
         zeros = keep.tile([P, P], F32)
         nc.vector.memset(zeros[:], 0.0)
 
-        w_scales_first = keep.tile([P, PASSES, BANK], U8, align_bytes=64)
-        w_scales_rest = keep.tile([P, PASSES, COLS - BANK], U8, align_bytes=64)
-        nc.vector.memset(w_scales_first[:].bitcast(I32), 0)
-        nc.vector.memset(w_scales_rest[:].bitcast(I32), 0)
+        w_scales = []
+        for which in range(2):
+            planes = keep.tile([P, PASSES, COLS // 2], U8, align_bytes=64, name="w_scales%d" % which)
+            nc.vector.memset(planes[:].bitcast(I32), 0)
+            w_scales.append(planes)
 
         x_sb = keep.tile([P, PASSES, K_PASS], BF16)
         for g in range(PASSES):
@@ -123,22 +124,20 @@ def tile_attentionblock_pa_s_kernel(tc, x, W_qk_words, W_qk_scales, out_0, out_1
                 .rearrange("g p c -> p g c"),
             )
 
-        load_words(0, FIRST_GROUP)
-
-        def load_scales(planes, first, width):
+        def load_scales(which):
+            first = COLS // 2 * which
             for r in range(4):
                 nc.sync.dma_start(
-                    out=planes[r:P:32].bitcast(I32),
-                    in_=W_qk_scales[:, r:16:4, first : first + width]
+                    out=w_scales[which][r:P:32].bitcast(I32),
+                    in_=W_qk_scales[:, r:16:4, first : first + COLS // 2]
                     .bitcast(I32)
                     .rearrange("g q n -> q g n"),
                 )
 
-        load_scales(w_scales_first, 0, BANK)
-        load_words(FIRST_GROUP, BANK - FIRST_GROUP)
-        load_scales(w_scales_rest, BANK, COLS - BANK)
-        for b in range(1, BANKS):
-            load_words(BANK * b, BANK)
+        for which in range(2):
+            load_scales(which)
+            for b in range(BANKS_PER_OUTPUT * which, BANKS_PER_OUTPUT * (which + 1)):
+                load_words(BANK * b, BANK)
 
         unread = psum.tile([P, P], F32)
 
@@ -183,13 +182,13 @@ def tile_attentionblock_pa_s_kernel(tc, x, W_qk_words, W_qk_scales, out_0, out_1
 
         def project(y, first, width, g):
             b, in_bank = divmod(first, BANK)
-            planes, offset = (w_scales_first, 0) if b == 0 else (w_scales_rest, BANK)
+            which, column = divmod(first, COLS // 2)
             nc.tensor.matmul_mx(
                 out=y,
                 lhsT=x_codes[:, g, :].bitcast(FP8X4),
                 lhsT_scale=x_scales[:, g, :],
                 rhs=w_words[:, b, g, 2 * in_bank : 2 * (in_bank + width)].bitcast(FP4X4),
-                rhs_scale=planes[:, g, first - offset : first - offset + width],
+                rhs_scale=w_scales[which][:, g, column : column + width],
                 start=(g == 0),
                 stop=(g == PASSES - 1),
             )

@@ -31,7 +31,7 @@ ROUND_MAGIC = 12582912.0
 
 HEADS = COLS // 2 // HEAD
 FIRST_GROUP = 2 * HEAD
-ROUNDS = ((2, 2, 0), (4, 1, 2), (4, 1, 2), (2, 0, 2))
+ROUNDS = ((2, 2, 0), (4, 2, 1), (4, 2, 1), (2, 0, 2))
 PIECES = 10
 FIRST = 8
 IDLE_BEFORE_X = 4
@@ -231,30 +231,40 @@ def tile_attentionblock_pa_s_kernel(tc, x, W_qk_words, W_qk_scales, out_0, out_1
             )
             return products
 
-        def add_and_store(adder, first_head, heads, products):
+        def add(adder, first_head, heads, products):
             rotated = work.tile([P, heads * HEAD], F32, name="rotated")
+            rotated_pieces[first_head] = rotated
             adder.tensor_tensor(
                 out=rotated[:].rearrange("p (m e) -> p m e", e=2),
                 in0=products[:, 0, :].rearrange("p (m e) -> p m e", e=2),
                 in1=products[:, 1, :].rearrange("p (m e) -> p m e", e=2)[:, :, ::-1],
                 op=ALU.add,
             )
-            which, head = divmod(first_head, HEADS)
-            out = (out_0, out_1)[which]
-            nc.sync.dma_start(
-                out=out[head : head + heads].rearrange("h n d -> n h d"),
-                in_=rotated[:].rearrange("n (h d) -> n h d", d=HEAD),
-            )
 
+        rotated_pieces = {}
         first_head = 0
+        late = []
         for heads, for_gpsimd, for_vector in ROUNDS:
             waiting = []
             for turn in range(for_gpsimd + for_vector):
                 products = multiply(first_head, heads)
+                for piece in late:
+                    add(nc.vector, *piece)
+                late = []
                 if turn < for_gpsimd:
-                    add_and_store(nc.gpsimd, first_head, heads, products)
+                    add(nc.gpsimd, first_head, heads, products)
                 else:
-                    waiting.append((first_head, products))
+                    waiting.append((first_head, heads, products))
                 first_head += heads
-            for late_head, products in waiting:
-                add_and_store(nc.vector, late_head, heads, products)
+            late = waiting
+        for piece in late:
+            add(nc.vector, *piece)
+
+        for first_head in sorted(rotated_pieces):
+            rotated = rotated_pieces[first_head]
+            heads = rotated.shape[1] // HEAD
+            which, head = divmod(first_head, HEADS)
+            nc.sync.dma_start(
+                out=(out_0, out_1)[which][head : head + heads].rearrange("h n d -> n h d"),
+                in_=rotated[:].rearrange("n (h d) -> n h d", d=HEAD),
+            )

@@ -34,7 +34,7 @@ FIRST_GROUP = 2 * HEAD
 ROUNDS = ((2, 2, 0), (4, 2, 1), (4, 2, 1), (2, 0, 2))
 PIECES = 10
 FIRST = 8
-IDLE_BEFORE_X = 4
+IDLE_BEFORE_X = 3
 IDLE_BEFORE_CODES = 2
 
 FLOPS = 2 * P * K * COLS
@@ -52,6 +52,10 @@ def build_angles(nc, pool, position):
             out=turns[:, 1, i : i + FIRST], in0=turns[:, 1, 0:FIRST], scalar1=ratio**i
         )
     nc.vector.tensor_scalar_add(out=turns[:, 0, :], in0=turns[:, 1, :], scalar1=0.25)
+    return turns
+
+
+def nearest_whole(nc, pool, turns):
     whole = pool.tile([P, 2, PAIRS], F32)
     nc.vector.tensor_scalar(
         out=whole[:],
@@ -61,9 +65,7 @@ def build_angles(nc, pool, position):
         op0=ALU.add,
         op1=ALU.subtract,
     )
-    part = pool.tile([P, 2, PAIRS], F32)
-    nc.vector.tensor_tensor(out=part[:], in0=turns[:], in1=whole[:], op=ALU.subtract)
-    return part
+    return whole
 
 
 def build_rotation_table(nc, pool, part):
@@ -149,7 +151,7 @@ def tile_attentionblock_pa_s_kernel(tc, x, W_qk_words, W_qk_scales, out_0, out_1
 
         identity = keep.tile([P, P], F32)
         make_identity(nc, identity[:])
-        part = build_angles(nc, keep, position)
+        turns = build_angles(nc, keep, position)
         unused = keep.tile([P, 1], F32)
         nc.scalar.activation(out=unused[:], in_=position[:], func=ACT.Sin, scale=0.0)
 
@@ -172,13 +174,20 @@ def tile_attentionblock_pa_s_kernel(tc, x, W_qk_words, W_qk_scales, out_0, out_1
             else:
                 nc.scalar.copy(out=side_by_side, in_=alternately)
         idle_matmuls(IDLE_BEFORE_CODES)
-        table = build_rotation_table(nc, keep, part)
-        for g in range(PASSES):
+
+        def quantise(g):
             nc.vector.quantize_mx(
                 out=x_codes[:, g, :].bitcast(FP8X4),
                 scales=x_scales[:, g, :],
                 in_=grouped[:, g, :],
             )
+
+        whole = nearest_whole(nc, keep, turns)
+        quantise(0)
+        part = keep.tile([P, 2, PAIRS], F32)
+        nc.vector.tensor_tensor(out=part[:], in0=turns[:], in1=whole[:], op=ALU.subtract)
+        quantise(1)
+        table = build_rotation_table(nc, keep, part)
 
         def project(y, first, width, g):
             b, in_bank = divmod(first, BANK)

@@ -115,16 +115,19 @@ def tile_attentionblock_pa_s_kernel(tc, x, W_qk_words, W_qk_scales, out_0, out_1
         for g in range(PASSES):
             nc.sync.dma_start(out=x_sb[:, g, :], in_=x[:, K_PASS * g : K_PASS * (g + 1)])
 
-        w_words = keep.tile([P, BANKS, PASSES, 2 * BANK], U8, align_bytes=64)
+        w_words = []
 
         def load_words(first, width):
-            b, in_bank = divmod(first, BANK)
+            words = keep.tile(
+                [P, PASSES, 2 * width], U8, align_bytes=64, name="w_words%d" % first
+            )
             nc.sync.dma_start(
-                out=w_words[:, b, :, 2 * in_bank : 2 * (in_bank + width)].bitcast(I32),
+                out=words[:].bitcast(I32),
                 in_=W_qk_words[:, :, 2 * first : 2 * (first + width)]
                 .bitcast(I32)
                 .rearrange("g p c -> p g c"),
             )
+            w_words.append((first, words))
 
         def load_scales(which):
             first = COLS // 2 * which
@@ -136,10 +139,13 @@ def tile_attentionblock_pa_s_kernel(tc, x, W_qk_words, W_qk_scales, out_0, out_1
                     .rearrange("g q n -> q g n"),
                 )
 
-        for which in range(2):
-            load_scales(which)
-            for b in range(BANKS_PER_OUTPUT * which, BANKS_PER_OUTPUT * (which + 1)):
-                load_words(BANK * b, BANK)
+        load_words(0, FIRST_GROUP)
+        load_scales(0)
+        load_words(FIRST_GROUP, BANK - FIRST_GROUP)
+        load_words(BANK, BANK)
+        load_scales(1)
+        for b in range(BANKS_PER_OUTPUT, BANKS):
+            load_words(BANK * b, BANK)
 
         unread = psum.tile([P, P], F32)
 
@@ -190,13 +196,14 @@ def tile_attentionblock_pa_s_kernel(tc, x, W_qk_words, W_qk_scales, out_0, out_1
         table = build_rotation_table(nc, keep, part)
 
         def project(y, first, width, g):
-            b, in_bank = divmod(first, BANK)
             which, column = divmod(first, COLS // 2)
+            loaded, words = [load for load in w_words if load[0] <= first][-1]
+            offset = 2 * (first - loaded)
             nc.tensor.matmul_mx(
                 out=y,
                 lhsT=x_codes[:, g, :].bitcast(FP8X4),
                 lhsT_scale=x_scales[:, g, :],
-                rhs=w_words[:, b, g, 2 * in_bank : 2 * (in_bank + width)].bitcast(FP4X4),
+                rhs=words[:, g, offset : offset + 2 * width].bitcast(FP4X4),
                 rhs_scale=w_scales[which][:, g, column : column + width],
                 start=(g == 0),
                 stop=(g == PASSES - 1),

@@ -31,7 +31,7 @@ ROUND_MAGIC = 12582912.0
 
 HEADS = COLS // 2 // HEAD
 FIRST_GROUP = 2 * HEAD
-ROUNDS = ((2, 2, 0), (4, 2, 1), (4, 2, 1), (2, 0, 2))
+ROUNDS = ((2, 2, 0), (4, 1, 1), (4, 2, 2), (2, 0, 2))
 PIECES = 10
 FIRST = 8
 IDLE_BEFORE_X = 3
@@ -272,9 +272,11 @@ def tile_attentionblock_pa_s_kernel(tc, x, W_qk_words, W_qk_scales, out_0, out_1
                 else:
                     waiting.append((first_head, heads, products))
                 first_head += heads
-            late = waiting
-        for piece in late:
-            add(nc.vector, *piece)
+            if len(waiting) == 1:
+                late = waiting
+            else:
+                for piece in waiting:
+                    add(nc.vector, *piece)
 
         for first_head in sorted(rotated_pieces):
             rotated = rotated_pieces[first_head]

@@ -33,6 +33,7 @@ HEADS = COLS // 2 // HEAD
 FIRST_GROUP = 2 * HEAD
 ROUNDS = ((2, 2, 0), (4, 1, 1), (4, 2, 2), (2, 0, 2))
 PIECES = 10
+STORES = (4, 4, 4, 4, 4, 4, 4, 2, 2)
 FIRST = 8
 IDLE_BEFORE_X = 3
 IDLE_BEFORE_CODES = 2
@@ -147,7 +148,7 @@ def tile_attentionblock_pa_s_kernel(tc, x, W_qk_words, W_qk_scales, out_0, out_1
         for b in range(BANKS_PER_OUTPUT, BANKS):
             load_words(BANK * b, BANK)
 
-        unread = psum.tile([P, P], F32)
+        unread = psum.tile([P, P], F32, tag="unread", name="unread")
 
         def idle_matmuls(count):
             for idle in range(count):
@@ -158,6 +159,7 @@ def tile_attentionblock_pa_s_kernel(tc, x, W_qk_words, W_qk_scales, out_0, out_1
         identity = keep.tile([P, P], F32)
         make_identity(nc, identity[:])
         turns = build_angles(nc, keep, position)
+        whole = nearest_whole(nc, keep, turns)
         unused = keep.tile([P, 1], F32)
         nc.scalar.activation(out=unused[:], in_=position[:], func=ACT.Sin, scale=0.0)
 
@@ -188,10 +190,9 @@ def tile_attentionblock_pa_s_kernel(tc, x, W_qk_words, W_qk_scales, out_0, out_1
                 in_=grouped[:, g, :],
             )
 
-        whole = nearest_whole(nc, keep, turns)
-        quantise(0)
         part = keep.tile([P, 2, PAIRS], F32)
         nc.vector.tensor_tensor(out=part[:], in0=turns[:], in1=whole[:], op=ALU.subtract)
+        quantise(0)
         quantise(1)
         table = build_rotation_table(nc, keep, part)
 
@@ -210,17 +211,20 @@ def tile_attentionblock_pa_s_kernel(tc, x, W_qk_words, W_qk_scales, out_0, out_1
             )
 
         y_first = psum.tile([P, FIRST_GROUP], F32)
-        y_rest = psum.tile([P, BANK - FIRST_GROUP], F32)
-        project(y_first[:], 0, FIRST_GROUP, 0)
-        project(y_rest[:, 0:FIRST_GROUP], FIRST_GROUP, FIRST_GROUP, 0)
-        project(y_first[:], 0, FIRST_GROUP, 1)
-        project(y_rest[:, 0:FIRST_GROUP], FIRST_GROUP, FIRST_GROUP, 1)
+        y_second = psum.tile([P, FIRST_GROUP], F32)
+        y_rest = psum.tile([P, BANK - 2 * FIRST_GROUP], F32)
+        for g in range(PASSES):
+            project(y_first[:], 0, FIRST_GROUP, g)
+        for g in range(PASSES):
+            project(y_second[:], FIRST_GROUP, FIRST_GROUP, g)
         for first in range(2 * FIRST_GROUP, BANK, FIRST_GROUP):
             for g in range(PASSES):
-                project(y_rest[:, first - FIRST_GROUP : first], first, FIRST_GROUP, g)
+                in_rest = first - 2 * FIRST_GROUP
+                project(y_rest[:, in_rest : in_rest + FIRST_GROUP], first, FIRST_GROUP, g)
         y_banks = [None]
         for b in range(1, BANKS):
-            y = psum.tile([P, BANK], F32, name="y%d" % b)
+            tag = "unread" if b == BANKS - 1 else "y%d" % b
+            y = psum.tile([P, BANK], F32, name="y%d" % b, tag=tag)
             for g in range(PASSES):
                 project(y[:], BANK * b, BANK, g)
             y_banks.append(y)
@@ -228,8 +232,10 @@ def tile_attentionblock_pa_s_kernel(tc, x, W_qk_words, W_qk_scales, out_0, out_1
         def y_columns(first, width):
             if first < FIRST_GROUP:
                 return y_first[:, first : first + width]
+            if first < 2 * FIRST_GROUP:
+                return y_second[:, first - FIRST_GROUP : first - FIRST_GROUP + width]
             if first < BANK:
-                return y_rest[:, first - FIRST_GROUP : first - FIRST_GROUP + width]
+                return y_rest[:, first - 2 * FIRST_GROUP : first - 2 * FIRST_GROUP + width]
             b, in_bank = divmod(first, BANK)
             return y_banks[b][:, in_bank : in_bank + width]
 
@@ -248,16 +254,15 @@ def tile_attentionblock_pa_s_kernel(tc, x, W_qk_words, W_qk_scales, out_0, out_1
             return products
 
         def add(adder, first_head, heads, products):
-            rotated = work.tile([P, heads * HEAD], F32, name="rotated")
-            rotated_pieces[first_head] = rotated
+            columns = rotated[:, HEAD * first_head : HEAD * (first_head + heads)]
             adder.tensor_tensor(
-                out=rotated[:].rearrange("p (m e) -> p m e", e=2),
+                out=columns.rearrange("p (m e) -> p m e", e=2),
                 in0=products[:, 0, :].rearrange("p (m e) -> p m e", e=2),
                 in1=products[:, 1, :].rearrange("p (m e) -> p m e", e=2)[:, :, ::-1],
                 op=ALU.add,
             )
 
-        rotated_pieces = {}
+        rotated = keep.tile([P, COLS], F32)
         first_head = 0
         late = []
         for heads, for_gpsimd, for_vector in ROUNDS:
@@ -278,11 +283,12 @@ def tile_attentionblock_pa_s_kernel(tc, x, W_qk_words, W_qk_scales, out_0, out_1
                 for piece in waiting:
                     add(nc.vector, *piece)
 
-        for first_head in sorted(rotated_pieces):
-            rotated = rotated_pieces[first_head]
-            heads = rotated.shape[1] // HEAD
+        first_head = 0
+        for heads in STORES:
             which, head = divmod(first_head, HEADS)
+            columns = rotated[:, HEAD * first_head : HEAD * (first_head + heads)]
             nc.sync.dma_start(
                 out=(out_0, out_1)[which][head : head + heads].rearrange("h n d -> n h d"),
-                in_=rotated[:].rearrange("n (h d) -> n h d", d=HEAD),
+                in_=columns.rearrange("n (h d) -> n h d", d=HEAD),
             )
+            first_head += heads

import math

import concourse.mybir as mybir
from concourse.masks import make_identity

F32 = mybir.dt.float32
BF16 = mybir.dt.bfloat16
I32 = mybir.dt.int32
U32 = mybir.dt.uint32
U8 = mybir.dt.uint8
FP8X4 = mybir.dt.float8_e4m3fn_x4
FP4X4 = mybir.dt.float4_e2m1fn_x4
ALU = mybir.AluOpType
ACT = mybir.ActivationFunctionType

P = 128
K = 1024
PACK = 4
K_PASS = P * PACK
PASSES = K // K_PASS
COLS = 2048
BANK = 512
BANKS = COLS // BANK
HEAD = 64
PAIRS = HEAD // 2
HEADS_IN_BANK = BANK // HEAD
BANKS_PER_OUTPUT = BANKS // 2

ROPE_BASE = 10000.0
ROUND_MAGIC = 12582912.0

HEADS = COLS // 2 // HEAD
FIRST_GROUP = 2 * HEAD
ROUNDS = ((2, 2, 0), (4, 1, 1), (4, 2, 2), (2, 0, 2))
PIECES = 10
STORES = (4, 4, 4, 4, 4, 4, 4, 2, 2)
FIRST = 8
IDLE_BEFORE_X = 3
IDLE_BEFORE_CODES = 2

FLOPS = 2 * P * K * COLS


def build_angles(nc, pool, position):
    turns = pool.tile([P, 2, PAIRS], F32)
    ratio = ROPE_BASE ** (-1.0 / PAIRS)
    for i in range(FIRST):
        nc.vector.tensor_scalar_mul(
            out=turns[:, 1, i : i + 1], in0=position[:], scalar1=ratio**i / (2.0 * math.pi)
        )
    for i in range(FIRST, PAIRS, FIRST):
        nc.vector.tensor_scalar_mul(
            out=turns[:, 1, i : i + FIRST], in0=turns[:, 1, 0:FIRST], scalar1=ratio**i
        )
    nc.vector.tensor_scalar_add(out=turns[:, 0, :], in0=turns[:, 1, :], scalar1=0.25)
    return turns


def nearest_whole(nc, pool, turns):
    whole = pool.tile([P, 2, PAIRS], F32)
    nc.vector.tensor_scalar(
        out=whole[:],
        in0=turns[:],
        scalar1=ROUND_MAGIC,
        scalar2=ROUND_MAGIC,
        op0=ALU.add,
        op1=ALU.subtract,
    )
    return whole


def build_rotation_table(nc, pool, part):
    table = pool.tile([P, 2, PAIRS, 2], F32)
    nc.scalar.activation(
        out=table[:, 0, :, :],
        in_=part[:, 0, :].unsqueeze(2).to_broadcast([P, PAIRS, 2]),
        func=ACT.Sin,
        scale=2.0 * math.pi,
    )
    nc.scalar.activation(
        out=table[:, 1, :, 0], in_=part[:, 1, :], func=ACT.Sin, scale=2.0 * math.pi
    )
    nc.scalar.activation(
        out=table[:, 1, :, 1], in_=part[:, 1, :], func=ACT.Sin, scale=-2.0 * math.pi
    )
    return table


def tile_attentionblock_pa_s_kernel(tc, x, W_qk_words, W_qk_scales, out_0, out_1):
    nc = tc.nc
    with (
        tc.tile_pool(name="keep", bufs=1) as keep,
        tc.tile_pool(name="work", bufs=PIECES) as work,
        tc.psum_pool(name="psum", bufs=1) as psum,
        tc.manual_schedule(),
    ):
        position = keep.tile([P, 1], F32)
        nc.gpsimd.iota(
            position[:],
            pattern=[[0, 1]],
            base=0,
            channel_multiplier=1,
            allow_small_or_imprecise_dtypes=True,
        )

        zeros = keep.tile([P, P], F32)
        nc.vector.memset(zeros[:], 0.0)

        w_scales = []
        for which in range(2):
            planes = keep.tile([P, PASSES, COLS // 2], U8, align_bytes=64, name="w_scales%d" % which)
            nc.vector.memset(planes[:].bitcast(I32), 0)
            w_scales.append(planes)

        x_sb = keep.tile([P, PASSES, K_PASS], BF16)
        for g in range(PASSES):
            nc.sync.dma_start(out=x_sb[:, g, :], in_=x[:, K_PASS * g : K_PASS * (g + 1)])

        w_words = []

        def load_words(first, width):
            words = keep.tile(
                [P, PASSES, 2 * width], U8, align_bytes=64, name="w_words%d" % first
            )
            nc.sync.dma_start(
                out=words[:].bitcast(I32),
                in_=W_qk_words[:, :, 2 * first : 2 * (first + width)]
                .bitcast(I32)
                .rearrange("g p c -> p g c"),
            )
            w_words.append((first, words))

        def load_scales(which):
            first = COLS // 2 * which
            for r in range(4):
                nc.sync.dma_start(
                    out=w_scales[which][r:P:32].bitcast(I32),
                    in_=W_qk_scales[:, r:16:4, first : first + COLS // 2]
                    .bitcast(I32)
                    .rearrange("g q n -> q g n"),
                )

        load_words(0, FIRST_GROUP)
        load_scales(0)
        load_words(FIRST_GROUP, BANK - FIRST_GROUP)
        load_words(BANK, BANK)
        load_scales(1)
        for b in range(BANKS_PER_OUTPUT, BANKS):
            load_words(BANK * b, BANK)

        unread = psum.tile([P, P], F32, tag="unread", name="unread")

        def idle_matmuls(count):
            for idle in range(count):
                nc.tensor.matmul(out=unread[:], lhsT=zeros[:], rhs=zeros[:], start=True, stop=True)

        idle_matmuls(IDLE_BEFORE_X)

        identity = keep.tile([P, P], F32)
        make_identity(nc, identity[:])
        turns = build_angles(nc, keep, position)
        whole = nearest_whole(nc, keep, turns)
        unused = keep.tile([P, 1], F32)
        nc.scalar.activation(out=unused[:], in_=position[:], func=ACT.Sin, scale=0.0)

        x_pairs = x_sb[:].bitcast(F32)
        grouped = keep.tile([P, PASSES, P * PACK], BF16, align_bytes=64)
        x_codes = keep.tile([P, PASSES, P], U32, align_bytes=64)
        x_scales = keep.tile([P, PASSES, P], U8, align_bytes=64)
        for g in range(PASSES):
            flipped = psum.tile([P, 2, P], F32, name="flipped%d" % g)
            for u in range(2):
                nc.tensor.transpose(
                    flipped[:, u, :],
                    x_pairs[:, g, u : K_PASS // 2 : 2],
                    identity[:],
                )
            side_by_side = grouped[:, g, :].bitcast(F32).rearrange("p (n u) -> p n u", u=2)
            alternately = flipped[:].rearrange("p u n -> p n u")
            if g == 0:
                nc.vector.tensor_copy(out=side_by_side, in_=alternately)
            else:
                nc.scalar.copy(out=side_by_side, in_=alternately)
        idle_matmuls(IDLE_BEFORE_CODES)

        def quantise(g):
            nc.vector.quantize_mx(
                out=x_codes[:, g, :].bitcast(FP8X4),
                scales=x_scales[:, g, :],
                in_=grouped[:, g, :],
            )

        part = keep.tile([P, 2, PAIRS], F32)
        nc.vector.tensor_tensor(out=part[:], in0=turns[:], in1=whole[:], op=ALU.subtract)
        quantise(0)
        quantise(1)
        table = build_rotation_table(nc, keep, part)

        def project(y, first, width, g):
            which, column = divmod(first, COLS // 2)
            loaded, words = [load for load in w_words if load[0] <= first][-1]
            offset = 2 * (first - loaded)
            nc.tensor.matmul_mx(
                out=y,
                lhsT=x_codes[:, g, :].bitcast(FP8X4),
                lhsT_scale=x_scales[:, g, :],
                rhs=words[:, g, offset : offset + 2 * width].bitcast(FP4X4),
                rhs_scale=w_scales[which][:, g, column : column + width],
                start=(g == 0),
                stop=(g == PASSES - 1),
            )

        y_first = psum.tile([P, FIRST_GROUP], F32)
        y_second = psum.tile([P, FIRST_GROUP], F32)
        y_rest = psum.tile([P, BANK - 2 * FIRST_GROUP], F32)
        for g in range(PASSES):
            project(y_first[:], 0, FIRST_GROUP, g)
        for g in range(PASSES):
            project(y_second[:], FIRST_GROUP, FIRST_GROUP, g)
        for first in range(2 * FIRST_GROUP, BANK, FIRST_GROUP):
            for g in range(PASSES):
                in_rest = first - 2 * FIRST_GROUP
                project(y_rest[:, in_rest : in_rest + FIRST_GROUP], first, FIRST_GROUP, g)
        y_banks = [None]
        for b in range(1, BANKS):
            tag = "unread" if b == BANKS - 1 else "y%d" % b
            y = psum.tile([P, BANK], F32, name="y%d" % b, tag=tag)
            for g in range(PASSES):
                project(y[:], BANK * b, BANK, g)
            y_banks.append(y)

        def y_columns(first, width):
            if first < FIRST_GROUP:
                return y_first[:, first : first + width]
            if first < 2 * FIRST_GROUP:
                return y_second[:, first - FIRST_GROUP : first - FIRST_GROUP + width]
            if first < BANK:
                return y_rest[:, first - 2 * FIRST_GROUP : first - 2 * FIRST_GROUP + width]
            b, in_bank = divmod(first, BANK)
            return y_banks[b][:, in_bank : in_bank + width]

        def multiply(first_head, heads):
            shape = [P, 2, heads, HEAD]
            products = work.tile([P, 2, heads * HEAD], F32, name="products")
            nc.vector.tensor_tensor(
                out=products[:].rearrange("p t (h d) -> p t h d", d=HEAD),
                in0=y_columns(HEAD * first_head, HEAD * heads)
                .rearrange("p (h d) -> p h d", d=HEAD)
                .unsqueeze(1)
                .to_broadcast(shape),
                in1=table[:].rearrange("p t i e -> p t (i e)").unsqueeze(2).to_broadcast(shape),
                op=ALU.mult,
            )
            return products

        def add(adder, first_head, heads, products):
            columns = rotated[:, HEAD * first_head : HEAD * (first_head + heads)]
            adder.tensor_tensor(
                out=columns.rearrange("p (m e) -> p m e", e=2),
                in0=products[:, 0, :].rearrange("p (m e) -> p m e", e=2),
                in1=products[:, 1, :].rearrange("p (m e) -> p m e", e=2)[:, :, ::-1],
                op=ALU.add,
            )

        rotated = keep.tile([P, COLS], F32)
        first_head = 0
        late = []
        for heads, for_gpsimd, for_vector in ROUNDS:
            waiting = []
            for turn in range(for_gpsimd + for_vector):
                products = multiply(first_head, heads)
                for piece in late:
                    add(nc.vector, *piece)
                late = []
                if turn < for_gpsimd:
                    add(nc.gpsimd, first_head, heads, products)
                else:
                    waiting.append((first_head, heads, products))
                first_head += heads
            if len(waiting) == 1:
                late = waiting
            else:
                for piece in waiting:
                    add(nc.vector, *piece)

        first_head = 0
        for heads in STORES:
            which, head = divmod(first_head, HEADS)
            columns = rotated[:, HEAD * first_head : HEAD * (first_head + heads)]
            nc.sync.dma_start(
                out=(out_0, out_1)[which][head : head + heads].rearrange("h n d -> n h d"),
                in_=columns.rearrange("n (h d) -> n h d", d=HEAD),
            )
            first_head += heads
